import numpy as np
import ml_dtypes


def mxq(x, axis, fmt="e4m3"):
    dtype, down = {"e4m3": (ml_dtypes.float8_e4m3fn, 7), "e5m2": (ml_dtypes.float8_e5m2, 14)}[fmt]
    v = np.moveaxis(np.asarray(x, np.float32).astype(ml_dtypes.bfloat16).astype(np.float64), axis, -1)
    blocks = v.reshape(v.shape[:-1] + (-1, 32))
    amax = np.abs(blocks).max(-1, keepdims=True)
    byte = np.maximum(np.where(amax > 0, np.frexp(amax)[1] - 1 + 127, 0) - down, 1)
    scale = np.exp2(byte - 127.0)
    codes = (blocks / scale).astype(np.float32).astype(dtype).astype(np.float64)
    return np.moveaxis((codes * scale).reshape(v.shape), -1, axis)


WIDE = False


def mx_kscale(k):
    if not WIDE:
        return np.ones(k)
    levels = np.array([20, -20, 10, -10, 0])
    a = np.random.permutation(np.resize(levels, k // 512 * 4)).reshape(k // 512, 4)
    idx = np.arange(k)
    return np.exp2(a[idx // 512, idx % 128 // 32])


BF16 = ml_dtypes.bfloat16


def bf(x):
    return np.asarray(x, np.float32).astype(BF16)


def f64(x):
    return np.asarray(x).astype(np.float64)


TAU = 1.0

S, B, C, F, W, H, K = 1, 2, 512, 512, 64, 48, 3


def _wsum(weight, epsilon):
    eps = f64(epsilon)
    delta = 0.5 * np.log(eps / (1.0 - eps))
    relaxed_weights = np.tanh((f64(weight) + delta) / TAU)
    return relaxed_weights.sum(axis=(3, 4))


def setup_inputs():
    s = mx_kscale(F)
    t = s / s.max()
    x = bf(np.random.standard_normal((B, C, W, H)) * 0.05)
    z = np.random.standard_normal((F, C, K, K)) * 0.5
    weight = bf(np.where(t[:, None, None, None] < 1, (2 * np.round(z * 4 - 0.5) + 1) / 8, z) * t[:, None, None, None])
    epsilon = bf(0.5 + (np.random.uniform(0.01, 0.99, (S, F, C, K, K)) - 0.5) * t[:, None, None, None])
    g = np.random.standard_normal((S, B, F, W, H)) * np.exp2(np.random.randint(-12, 1, (S, B, 1, W, H)))
    g = g / t[:, None, None]
    return {"x": x, "weight": weight, "epsilon": epsilon, "grad_out": bf(g)}


def reference(x, weight, epsilon, grad_out):
    wsum = _wsum(weight, epsilon)
    g = f64(grad_out)
    s_, b_, f_, w_, h_ = g.shape
    c_ = wsum.shape[2]
    wq = mxq(wsum, 1, "e4m3")
    gq = mxq(g.reshape(s_, b_, f_, w_ * h_), 2, "e5m2")
    gx = wq.transpose(0, 2, 1)[:, None] @ gq
    return gx.sum(axis=0).reshape(b_, c_, w_, h_)

@@ -1,0 +1,258 @@
+import concourse.mybir as mybir
+from concourse.masks import make_identity
+
+F32 = mybir.dt.float32
+BF16 = mybir.dt.bfloat16
+U32 = mybir.dt.uint32
+U8 = mybir.dt.uint8
+E4X4 = mybir.dt.float8_e4m3fn_x4
+E5X4 = mybir.dt.float8_e5m2_x4
+ACT = mybir.ActivationFunctionType
+ALU = mybir.AluOpType
+AX = mybir.AxisListType
+
+P = 128
+PACK = 4
+NF = 512
+NC = 512
+KK = 9
+NB = 2
+NPOS = 3072
+HC = 64
+HW = HC * KK
+NCH = NC // HC
+GW = 1024
+NG = NB * NPOS // GW
+NBANK = 512
+
+FLOPS = 2 * NF * NC * NB * NPOS
+BYTES = 2 * (NF * NC * KK * 2) + NB * NF * NPOS * 2 + NB * NC * NPOS * 4
+
+
+def tile_bibayesianconv_kernel(tc, x, weight, epsilon, grad_out, out):
+    nc = tc.nc
+    w_v = weight.rearrange("(p t) c k l -> p t (c k l)", t=PACK)
+    e_v = epsilon.rearrange("s (p t) c k l -> (s p) t (c k l)", t=PACK)
+    g_v = grad_out.rearrange("s b (p t) w h -> p (s b) t (w h)", t=PACK)
+    o_v = out.rearrange("b (m c) w h -> c b m (w h)", c=P)
+    CHUNK = PACK * HW
+
+    with tc.manual_schedule(), tc.tile_pool(name="keep", bufs=1) as keep:
+        z = [keep.tile([P, PACK, HW], F32, name="z%d" % i) for i in range(NCH)]
+        gq = keep.tile([P, NB * NPOS], U32, name="gq", align_bytes=64)
+        gs = keep.tile([P, NB * NPOS], U8, name="gs", align_bytes=64)
+        wq = keep.tile([P, NC], U32, name="wq", align_bytes=64)
+        ws = keep.tile([P, NC], U8, name="ws", align_bytes=64)
+        idf = keep.tile([P, P], F32, name="idf")
+        halfp = keep.tile([P, P], F32, name="halfp")
+        halfn = keep.tile([P, P], F32, name="halfn")
+        idb = keep.tile([P, P], BF16, name="idb")
+        w_of = {}
+        l2s = {}
+        wgrp = {}
+
+        make_identity(nc, idf[:])
+        make_identity(nc, idb[:])
+        nc.vector.tensor_scalar_mul(out=halfp[:], in0=idf[:], scalar1=0.5)
+        nc.vector.tensor_scalar_mul(out=halfn[:], in0=idf[:], scalar1=-0.5)
+
+        def load_wh(i):
+            t = keep.tile([P, PACK, HW], BF16, name="wh%d" % i, tag="wh", bufs=2)
+            nc.sync.dma_start(out=t[:], in_=w_v[:, :, i * HW:(i + 1) * HW])
+            w_of[i] = t[:]
+
+        def load_w(m):
+            t = keep.tile([P, PACK, 2 * HW], BF16, name="w%d" % m, tag="w", bufs=2)
+            nc.sync.dma_start(out=t[:], in_=w_v[:, :, m * 2 * HW:(m + 1) * 2 * HW])
+            w_of[2 * m] = t[:, :, 0:HW]
+            w_of[2 * m + 1] = t[:, :, HW:2 * HW]
+
+        def diff(i):
+            nc.vector.tensor_tensor(out=z[i][:], in0=z[i][:], in1=l2s[i][:], op=ALU.subtract)
+
+        def diff_pool(i):
+            for t0 in range(0, PACK, 2):
+                nc.gpsimd.tensor_tensor(
+                    out=z[i][:, t0:t0 + 2, :], in0=z[i][:, t0:t0 + 2, :], in1=l2s[i][:, t0:t0 + 2, :], op=ALU.subtract)
+
+        def add_w(i):
+            nc.vector.scalar_tensor_tensor(
+                out=z[i][:], in0=z[i][:], scalar=0.5, in1=w_of[i], op0=ALU.mult, op1=ALU.add)
+
+        def tanh(i):
+            nc.scalar.activation(out=z[i][:], in_=z[i][:], func=ACT.Tanh)
+
+        z0flat = z[0][:].rearrange("p t x -> p (t x)")
+        with tc.psum_pool(name="zp", bufs=1) as zp:
+            zbank = []
+            with tc.tile_pool(name="ph1", bufs=2) as ph1:
+                e_t = {}
+                graw = {}
+                ggrp = {}
+
+                def load_e(i):
+                    e_t[i] = ph1.tile([P, PACK, HW], BF16, name="e%d" % i, tag="e", bufs=3)
+                    nc.sync.dma_start(out=e_t[i][:], in_=e_v[:, :, i * HW:(i + 1) * HW])
+
+                def load_g(j, lo=0, hi=GW):
+                    if lo == 0:
+                        graw[j] = ph1.tile([P, PACK, GW], BF16, name="graw%d" % j, tag="graw", bufs=2)
+                    b, q = divmod(j, NPOS // GW)
+                    nc.sync.dma_start(out=graw[j][:, :, lo:hi], in_=g_v[:, b, :, q * GW + lo:q * GW + hi])
+
+                def regroup_g(j, lo=0, hi=GW):
+                    if lo == 0:
+                        ggrp[j] = ph1.tile([P, GW, PACK], BF16, name="ggrp%d" % j, tag="ggrp", bufs=2, align_bytes=64)
+                    nc.vector.tensor_copy(out=ggrp[j][:, lo:hi, :], in_=graw[j][:, :, lo:hi].rearrange("p t w -> p w t"))
+
+                def quant_g(j):
+                    nc.vector.quantize_mx(
+                        out=gq[:, j * GW:(j + 1) * GW].bitcast(E5X4), scales=gs[:, j * GW:(j + 1) * GW],
+                        in_=ggrp[j][:].rearrange("p w t -> p (w t)"))
+
+                def logs(i):
+                    nc.scalar.activation(out=z[i][:], in_=e_t[i][:], func=ACT.Ln)
+                    l2s[i] = keep.tile([P, PACK, HW], F32, name="l2_%d" % i, tag="l2", bufs=5)
+                    nc.scalar.activation(out=l2s[i][:], in_=e_t[i][:], func=ACT.Ln, scale=-1.0, bias=1.0)
+
+                def pe_z0():
+                    l2flat = l2s[0][:].rearrange("p t x -> p (t x)")
+                    wflat = w_of[0].rearrange("p t x -> p (t x)")
+                    for lo in range(0, CHUNK, NBANK):
+                        hi = min(lo + NBANK, CHUNK)
+                        zb = zp.tile([P, NBANK], F32, name="zb%d" % (lo // NBANK))
+                        zbank.append((zb, lo, hi))
+                        nc.tensor.matmul(out=zb[:, 0:hi - lo], lhsT=halfp[:], rhs=z0flat[:, lo:hi], start=True, stop=False)
+                        nc.tensor.matmul(out=zb[:, 0:hi - lo], lhsT=halfn[:], rhs=l2flat[:, lo:hi], start=False, stop=False)
+                        nc.tensor.matmul(out=zb[:, 0:hi - lo], lhsT=idb[:], rhs=wflat[:, lo:hi], start=False, stop=True)
+
+                load_g(0, 0, GW // 2)
+                load_e(0)
+                load_g(0, GW // 2, GW)
+                load_g(1)
+                load_e(1)
+                load_wh(0)
+                regroup_g(0, 0, GW // 2)
+                regroup_g(0, GW // 2, GW)
+                quant_g(0)
+                load_g(2)
+                load_e(2)
+                load_wh(1)
+                logs(0)
+                pe_z0()
+                load_e(3)
+                load_w(1)
+                logs(1)
+                load_e(4)
+                regroup_g(1)
+                quant_g(1)
+                load_g(3)
+                logs(2)
+                load_e(5)
+                load_w(2)
+                logs(3)
+                load_e(6)
+                regroup_g(2)
+                load_g(4)
+                logs(4)
+                load_e(7)
+                diff(1)
+                quant_g(2)
+                add_w(1)
+                diff(2)
+                add_w(2)
+                regroup_g(3)
+                load_g(5)
+                diff(3)
+                quant_g(3)
+                add_w(3)
+                load_w(3)
+                logs(5)
+                logs(6)
+                logs(7)
+                regroup_g(4)
+                diff(4)
+                quant_g(4)
+                add_w(4)
+                regroup_g(5)
+                quant_g(5)
+
+            for zb, lo, hi in zbank:
+                nc.scalar.activation(out=z0flat[:, lo:hi], in_=zb[:, 0:hi - lo], func=ACT.Tanh)
+
+        with tc.psum_pool(name="acc", bufs=8) as acc, tc.tile_pool(name="stage", bufs=6) as stg:
+            todo = []
+            state = {}
+
+            def sum9(i):
+                m, h = divmod(i, 2)
+                if h == 0:
+                    wgrp[m] = keep.tile([P, P, PACK], BF16, name="wgrp%d" % m, tag="wgrp", bufs=2, align_bytes=64)
+                with nc.allow_low_precision(reason="the float32 sum of 9 is rounded once to bfloat16 on the way out"):
+                    nc.vector.tensor_reduce(
+                        out=wgrp[m][:, h * HC:(h + 1) * HC, :].rearrange("p c t -> p t c"),
+                        in_=z[i][:].rearrange("p t (c k) -> p t c k", k=KK), axis=AX.X, op=ALU.add)
+
+            def quant_w(m):
+                cols = slice(m * P, (m + 1) * P)
+                nc.vector.quantize_mx(
+                    out=wq[:, cols].bitcast(E4X4), scales=ws[:, cols],
+                    in_=wgrp[m][:].rearrange("p c t -> p (c t)"))
+                for n in range(NB * NPOS // NBANK):
+                    todo.append((m, n))
+
+            def drain(engines):
+                for r in range(len(engines)):
+                    m, n = todo.pop(0)
+                    cols = slice(m * P, (m + 1) * P)
+                    if n % 2 == 0:
+                        state["st"] = stg.tile([P, 2 * NBANK], F32, name="st", tag="st")
+                    st = state["st"]
+                    ps = acc.tile([P, NBANK], F32, name="ps", tag="ps")
+                    nc.tensor.matmul_mx(
+                        out=ps[:], lhsT=wq[:, cols].bitcast(E4X4), lhsT_scale=ws[:, cols],
+                        rhs=gq[:, n * NBANK:(n + 1) * NBANK].bitcast(E5X4), rhs_scale=gs[:, n * NBANK:(n + 1) * NBANK],
+                        start=True, stop=True)
+                    half = st[:, (n % 2) * NBANK:(n % 2 + 1) * NBANK]
+                    if engines[r] == "v":
+                        nc.vector.tensor_copy(out=half, in_=ps[:])
+                    else:
+                        nc.scalar.copy(out=half, in_=ps[:])
+                    if n % 2 == 1:
+                        b, q = divmod(n // 2, NPOS // (2 * NBANK))
+                        nc.sync.dma_start(out=o_v[:, b, m, q * 2 * NBANK:(q + 1) * 2 * NBANK], in_=st[:])
+
+            diff_pool(5)
+            diff_pool(6)
+            diff_pool(7)
+            tanh(1)
+            tanh(2)
+            tanh(3)
+            tanh(4)
+            sum9(0)
+            sum9(1)
+            quant_w(0)
+            add_w(5)
+            drain("s" * 12)
+            sum9(2)
+            sum9(3)
+            quant_w(1)
+            add_w(6)
+            drain("ss")
+            tanh(5)
+            sum9(4)
+            drain("svsvv")
+            sum9(5)
+            quant_w(2)
+            drain("sss")
+            tanh(6)
+            drain("v")
+            add_w(7)
+            drain("s" * 5)
+            tanh(7)
+            drain("vv")
+            sum9(6)
+            drain("s" * 6)
+            sum9(7)
+            quant_w(3)
+            drain("sv" * 6)

@@ -70,11 +70,6 @@ def tile_bibayesianconv_kernel(tc, x, weight, epsilon, grad_out, out):
         def diff(i):
             nc.vector.tensor_tensor(out=z[i][:], in0=z[i][:], in1=l2s[i][:], op=ALU.subtract)
 
-        def diff_pool(i):
-            for t0 in range(0, PACK, 2):
-                nc.gpsimd.tensor_tensor(
-                    out=z[i][:, t0:t0 + 2, :], in0=z[i][:, t0:t0 + 2, :], in1=l2s[i][:, t0:t0 + 2, :], op=ALU.subtract)
-
         def add_w(i):
             nc.vector.scalar_tensor_tensor(
                 out=z[i][:], in0=z[i][:], scalar=0.5, in1=w_of[i], op0=ALU.mult, op1=ALU.add)
@@ -222,9 +217,6 @@ def tile_bibayesianconv_kernel(tc, x, weight, epsilon, grad_out, out):
                         b, q = divmod(n // 2, NPOS // (2 * NBANK))
                         nc.sync.dma_start(out=o_v[:, b, m, q * 2 * NBANK:(q + 1) * 2 * NBANK], in_=st[:])
 
-            diff_pool(5)
-            diff_pool(6)
-            diff_pool(7)
             tanh(1)
             tanh(2)
             tanh(3)
@@ -232,11 +224,13 @@ def tile_bibayesianconv_kernel(tc, x, weight, epsilon, grad_out, out):
             sum9(0)
             sum9(1)
             quant_w(0)
+            diff(5)
             add_w(5)
             drain("s" * 12)
             sum9(2)
             sum9(3)
             quant_w(1)
+            diff(6)
             add_w(6)
             drain("ss")
             tanh(5)
@@ -247,6 +241,7 @@ def tile_bibayesianconv_kernel(tc, x, weight, epsilon, grad_out, out):
             drain("sss")
             tanh(6)
             drain("v")
+            diff(7)
             add_w(7)
             drain("s" * 5)
             tanh(7)

@@ -70,6 +70,11 @@ def tile_bibayesianconv_kernel(tc, x, weight, epsilon, grad_out, out):
         def diff(i):
             nc.vector.tensor_tensor(out=z[i][:], in0=z[i][:], in1=l2s[i][:], op=ALU.subtract)
 
+        def diff_pool(i):
+            for t0 in range(0, PACK, 2):
+                nc.gpsimd.tensor_tensor(
+                    out=z[i][:, t0:t0 + 2, :], in0=z[i][:, t0:t0 + 2, :], in1=l2s[i][:, t0:t0 + 2, :], op=ALU.subtract)
+
         def add_w(i):
             nc.vector.scalar_tensor_tensor(
                 out=z[i][:], in0=z[i][:], scalar=0.5, in1=w_of[i], op0=ALU.mult, op1=ALU.add)
@@ -98,7 +103,9 @@ def tile_bibayesianconv_kernel(tc, x, weight, epsilon, grad_out, out):
                 def regroup_g(j, lo=0, hi=GW):
                     if lo == 0:
                         ggrp[j] = ph1.tile([P, GW, PACK], BF16, name="ggrp%d" % j, tag="ggrp", bufs=2, align_bytes=64)
-                    nc.vector.tensor_copy(out=ggrp[j][:, lo:hi, :], in_=graw[j][:, :, lo:hi].rearrange("p t w -> p w t"))
+                    nc.vector.tensor_copy(
+                        out=ggrp[j][:, lo:hi, :].rearrange("p (c i) t -> p c t i", i=4),
+                        in_=graw[j][:, :, lo:hi].rearrange("p t (c i) -> p c t i", i=4))
 
                 def quant_g(j):
                     nc.vector.quantize_mx(
@@ -217,6 +224,9 @@ def tile_bibayesianconv_kernel(tc, x, weight, epsilon, grad_out, out):
                         b, q = divmod(n // 2, NPOS // (2 * NBANK))
                         nc.sync.dma_start(out=o_v[:, b, m, q * 2 * NBANK:(q + 1) * 2 * NBANK], in_=st[:])
 
+            diff_pool(5)
+            diff_pool(6)
+            diff_pool(7)
             tanh(1)
             tanh(2)
             tanh(3)
@@ -224,13 +234,11 @@ def tile_bibayesianconv_kernel(tc, x, weight, epsilon, grad_out, out):
             sum9(0)
             sum9(1)
             quant_w(0)
-            diff(5)
             add_w(5)
             drain("s" * 12)
             sum9(2)
             sum9(3)
             quant_w(1)
-            diff(6)
             add_w(6)
             drain("ss")
             tanh(5)
@@ -241,7 +249,6 @@ def tile_bibayesianconv_kernel(tc, x, weight, epsilon, grad_out, out):
             drain("sss")
             tanh(6)
             drain("v")
-            diff(7)
             add_w(7)
             drain("s" * 5)
             tanh(7)

@@ -68,21 +68,31 @@ def tile_bibayesianconv_kernel(tc, x, weight, epsilon, grad_out, out):
             w_of[2 * m + 1] = t[:, :, HW:2 * HW]
 
         def diff(i):
-            nc.vector.tensor_tensor(out=z[i][:], in0=z[i][:], in1=l2s[i][:], op=ALU.subtract)
+            lo = PE_COLS.get(i, 0)
+            nc.vector.tensor_tensor(
+                out=zflat[i][:, lo:CHUNK], in0=zflat[i][:, lo:CHUNK],
+                in1=l2s[i][:].rearrange("p t x -> p (t x)")[:, lo:CHUNK], op=ALU.subtract)
 
         def diff_pool(i):
-            for t0 in range(0, PACK, 2):
+            for t0 in range(PACK):
                 nc.gpsimd.tensor_tensor(
-                    out=z[i][:, t0:t0 + 2, :], in0=z[i][:, t0:t0 + 2, :], in1=l2s[i][:, t0:t0 + 2, :], op=ALU.subtract)
+                    out=z[i][:, t0, :], in0=z[i][:, t0, :], in1=l2s[i][:, t0, :], op=ALU.subtract)
 
         def add_w(i):
+            if i == 1:
+                lo = PE_COLS[1]
+                nc.vector.scalar_tensor_tensor(
+                    out=zflat[1][:, lo:CHUNK], in0=zflat[1][:, lo:CHUNK], scalar=0.5,
+                    in1=w_of[1].rearrange("p t x -> p (t x)")[:, lo:CHUNK], op0=ALU.mult, op1=ALU.add)
+                return
             nc.vector.scalar_tensor_tensor(
                 out=z[i][:], in0=z[i][:], scalar=0.5, in1=w_of[i], op0=ALU.mult, op1=ALU.add)
 
         def tanh(i):
             nc.scalar.activation(out=z[i][:], in_=z[i][:], func=ACT.Tanh)
 
-        z0flat = z[0][:].rearrange("p t x -> p (t x)")
+        zflat = [t[:].rearrange("p t x -> p (t x)") for t in z]
+        PE_COLS = {0: CHUNK, 1: 768}
         with tc.psum_pool(name="zp", bufs=1) as zp:
             zbank = []
             with tc.tile_pool(name="ph1", bufs=2) as ph1:
@@ -117,14 +127,14 @@ def tile_bibayesianconv_kernel(tc, x, weight, epsilon, grad_out, out):
                     l2s[i] = keep.tile([P, PACK, HW], F32, name="l2_%d" % i, tag="l2", bufs=5)
                     nc.scalar.activation(out=l2s[i][:], in_=e_t[i][:], func=ACT.Ln, scale=-1.0, bias=1.0)
 
-                def pe_z0():
-                    l2flat = l2s[0][:].rearrange("p t x -> p (t x)")
-                    wflat = w_of[0].rearrange("p t x -> p (t x)")
-                    for lo in range(0, CHUNK, NBANK):
-                        hi = min(lo + NBANK, CHUNK)
-                        zb = zp.tile([P, NBANK], F32, name="zb%d" % (lo // NBANK))
-                        zbank.append((zb, lo, hi))
-                        nc.tensor.matmul(out=zb[:, 0:hi - lo], lhsT=halfp[:], rhs=z0flat[:, lo:hi], start=True, stop=False)
+                def pe_z(i):
+                    l2flat = l2s[i][:].rearrange("p t x -> p (t x)")
+                    wflat = w_of[i].rearrange("p t x -> p (t x)")
+                    for lo in range(0, PE_COLS[i], NBANK):
+                        hi = min(lo + NBANK, PE_COLS[i])
+                        zb = zp.tile([P, NBANK], F32, name="zb%d_%d" % (i, lo // NBANK))
+                        zbank.append((i, zb, lo, hi))
+                        nc.tensor.matmul(out=zb[:, 0:hi - lo], lhsT=halfp[:], rhs=zflat[i][:, lo:hi], start=True, stop=False)
                         nc.tensor.matmul(out=zb[:, 0:hi - lo], lhsT=halfn[:], rhs=l2flat[:, lo:hi], start=False, stop=False)
                         nc.tensor.matmul(out=zb[:, 0:hi - lo], lhsT=idb[:], rhs=wflat[:, lo:hi], start=False, stop=True)
 
@@ -141,10 +151,11 @@ def tile_bibayesianconv_kernel(tc, x, weight, epsilon, grad_out, out):
                 load_e(2)
                 load_wh(1)
                 logs(0)
-                pe_z0()
+                pe_z(0)
                 load_e(3)
                 load_w(1)
                 logs(1)
+                pe_z(1)
                 load_e(4)
                 regroup_g(1)
                 quant_g(1)
@@ -179,8 +190,9 @@ def tile_bibayesianconv_kernel(tc, x, weight, epsilon, grad_out, out):
                 regroup_g(5)
                 quant_g(5)
 
-            for zb, lo, hi in zbank:
-                nc.scalar.activation(out=z0flat[:, lo:hi], in_=zb[:, 0:hi - lo], func=ACT.Tanh)
+            for i, zb, lo, hi in zbank:
+                nc.scalar.activation(out=zflat[i][:, lo:hi], in_=zb[:, 0:hi - lo], func=ACT.Tanh)
+            nc.scalar.activation(out=zflat[1][:, PE_COLS[1]:CHUNK], in_=zflat[1][:, PE_COLS[1]:CHUNK], func=ACT.Tanh)
 
         with tc.psum_pool(name="acc", bufs=8) as acc, tc.tile_pool(name="stage", bufs=6) as stg:
             todo = []
@@ -227,7 +239,6 @@ def tile_bibayesianconv_kernel(tc, x, weight, epsilon, grad_out, out):
             diff_pool(5)
             diff_pool(6)
             diff_pool(7)
-            tanh(1)
             tanh(2)
             tanh(3)
             tanh(4)

@@ -68,31 +68,21 @@ def tile_bibayesianconv_kernel(tc, x, weight, epsilon, grad_out, out):
             w_of[2 * m + 1] = t[:, :, HW:2 * HW]
 
         def diff(i):
-            lo = PE_COLS.get(i, 0)
-            nc.vector.tensor_tensor(
-                out=zflat[i][:, lo:CHUNK], in0=zflat[i][:, lo:CHUNK],
-                in1=l2s[i][:].rearrange("p t x -> p (t x)")[:, lo:CHUNK], op=ALU.subtract)
+            nc.vector.tensor_tensor(out=z[i][:], in0=z[i][:], in1=l2s[i][:], op=ALU.subtract)
 
         def diff_pool(i):
-            for t0 in range(PACK):
+            for t0 in range(0, PACK, 2):
                 nc.gpsimd.tensor_tensor(
-                    out=z[i][:, t0, :], in0=z[i][:, t0, :], in1=l2s[i][:, t0, :], op=ALU.subtract)
+                    out=z[i][:, t0:t0 + 2, :], in0=z[i][:, t0:t0 + 2, :], in1=l2s[i][:, t0:t0 + 2, :], op=ALU.subtract)
 
         def add_w(i):
-            if i == 1:
-                lo = PE_COLS[1]
-                nc.vector.scalar_tensor_tensor(
-                    out=zflat[1][:, lo:CHUNK], in0=zflat[1][:, lo:CHUNK], scalar=0.5,
-                    in1=w_of[1].rearrange("p t x -> p (t x)")[:, lo:CHUNK], op0=ALU.mult, op1=ALU.add)
-                return
             nc.vector.scalar_tensor_tensor(
                 out=z[i][:], in0=z[i][:], scalar=0.5, in1=w_of[i], op0=ALU.mult, op1=ALU.add)
 
         def tanh(i):
             nc.scalar.activation(out=z[i][:], in_=z[i][:], func=ACT.Tanh)
 
-        zflat = [t[:].rearrange("p t x -> p (t x)") for t in z]
-        PE_COLS = {0: CHUNK, 1: 768}
+        z0flat = z[0][:].rearrange("p t x -> p (t x)")
         with tc.psum_pool(name="zp", bufs=1) as zp:
             zbank = []
             with tc.tile_pool(name="ph1", bufs=2) as ph1:
@@ -124,17 +114,20 @@ def tile_bibayesianconv_kernel(tc, x, weight, epsilon, grad_out, out):
 
                 def logs(i):
                     nc.scalar.activation(out=z[i][:], in_=e_t[i][:], func=ACT.Ln)
-                    l2s[i] = keep.tile([P, PACK, HW], F32, name="l2_%d" % i, tag="l2", bufs=5)
+                    if i == 0:
+                        l2s[i] = keep.tile([P, PACK, HW], F32, name="l2_0")
+                    else:
+                        l2s[i] = keep.tile([P, PACK, HW], F32, name="l2_%d" % i, tag="l2", bufs=4)
                     nc.scalar.activation(out=l2s[i][:], in_=e_t[i][:], func=ACT.Ln, scale=-1.0, bias=1.0)
 
-                def pe_z(i):
-                    l2flat = l2s[i][:].rearrange("p t x -> p (t x)")
-                    wflat = w_of[i].rearrange("p t x -> p (t x)")
-                    for lo in range(0, PE_COLS[i], NBANK):
-                        hi = min(lo + NBANK, PE_COLS[i])
-                        zb = zp.tile([P, NBANK], F32, name="zb%d_%d" % (i, lo // NBANK))
-                        zbank.append((i, zb, lo, hi))
-                        nc.tensor.matmul(out=zb[:, 0:hi - lo], lhsT=halfp[:], rhs=zflat[i][:, lo:hi], start=True, stop=False)
+                def pe_z0():
+                    l2flat = l2s[0][:].rearrange("p t x -> p (t x)")
+                    wflat = w_of[0].rearrange("p t x -> p (t x)")
+                    for lo in range(0, CHUNK, NBANK):
+                        hi = min(lo + NBANK, CHUNK)
+                        zb = zp.tile([P, NBANK], F32, name="zb%d" % (lo // NBANK))
+                        zbank.append((zb, lo, hi))
+                        nc.tensor.matmul(out=zb[:, 0:hi - lo], lhsT=halfp[:], rhs=z0flat[:, lo:hi], start=True, stop=False)
                         nc.tensor.matmul(out=zb[:, 0:hi - lo], lhsT=halfn[:], rhs=l2flat[:, lo:hi], start=False, stop=False)
                         nc.tensor.matmul(out=zb[:, 0:hi - lo], lhsT=idb[:], rhs=wflat[:, lo:hi], start=False, stop=True)
 
@@ -151,11 +144,10 @@ def tile_bibayesianconv_kernel(tc, x, weight, epsilon, grad_out, out):
                 load_e(2)
                 load_wh(1)
                 logs(0)
-                pe_z(0)
+                pe_z0()
                 load_e(3)
                 load_w(1)
                 logs(1)
-                pe_z(1)
                 load_e(4)
                 regroup_g(1)
                 quant_g(1)
@@ -190,9 +182,8 @@ def tile_bibayesianconv_kernel(tc, x, weight, epsilon, grad_out, out):
                 regroup_g(5)
                 quant_g(5)
 
-            for i, zb, lo, hi in zbank:
-                nc.scalar.activation(out=zflat[i][:, lo:hi], in_=zb[:, 0:hi - lo], func=ACT.Tanh)
-            nc.scalar.activation(out=zflat[1][:, PE_COLS[1]:CHUNK], in_=zflat[1][:, PE_COLS[1]:CHUNK], func=ACT.Tanh)
+            for zb, lo, hi in zbank:
+                nc.scalar.activation(out=z0flat[:, lo:hi], in_=zb[:, 0:hi - lo], func=ACT.Tanh)
 
         with tc.psum_pool(name="acc", bufs=8) as acc, tc.tile_pool(name="stage", bufs=6) as stg:
             todo = []
@@ -239,6 +230,7 @@ def tile_bibayesianconv_kernel(tc, x, weight, epsilon, grad_out, out):
             diff_pool(5)
             diff_pool(6)
             diff_pool(7)
+            tanh(1)
             tanh(2)
             tanh(3)
             tanh(4)

@@ -71,9 +71,9 @@ def tile_bibayesianconv_kernel(tc, x, weight, epsilon, grad_out, out):
             nc.vector.tensor_tensor(out=z[i][:], in0=z[i][:], in1=l2s[i][:], op=ALU.subtract)
 
         def diff_pool(i):
-            for t0 in range(0, PACK, 2):
+            for t0 in range(PACK):
                 nc.gpsimd.tensor_tensor(
-                    out=z[i][:, t0:t0 + 2, :], in0=z[i][:, t0:t0 + 2, :], in1=l2s[i][:, t0:t0 + 2, :], op=ALU.subtract)
+                    out=z[i][:, t0, :], in0=z[i][:, t0, :], in1=l2s[i][:, t0, :], op=ALU.subtract)
 
         def add_w(i):
             nc.vector.scalar_tensor_tensor(
@@ -114,10 +114,7 @@ def tile_bibayesianconv_kernel(tc, x, weight, epsilon, grad_out, out):
 
                 def logs(i):
                     nc.scalar.activation(out=z[i][:], in_=e_t[i][:], func=ACT.Ln)
-                    if i == 0:
-                        l2s[i] = keep.tile([P, PACK, HW], F32, name="l2_0")
-                    else:
-                        l2s[i] = keep.tile([P, PACK, HW], F32, name="l2_%d" % i, tag="l2", bufs=4)
+                    l2s[i] = keep.tile([P, PACK, HW], F32, name="l2_%d" % i, tag="l2", bufs=5)
                     nc.scalar.activation(out=l2s[i][:], in_=e_t[i][:], func=ACT.Ln, scale=-1.0, bias=1.0)
 
                 def pe_z0():

@@ -68,21 +68,31 @@ def tile_bibayesianconv_kernel(tc, x, weight, epsilon, grad_out, out):
             w_of[2 * m + 1] = t[:, :, HW:2 * HW]
 
         def diff(i):
-            nc.vector.tensor_tensor(out=z[i][:], in0=z[i][:], in1=l2s[i][:], op=ALU.subtract)
+            lo = PE_COLS.get(i, 0)
+            nc.vector.tensor_tensor(
+                out=zflat[i][:, lo:CHUNK], in0=zflat[i][:, lo:CHUNK],
+                in1=l2s[i][:].rearrange("p t x -> p (t x)")[:, lo:CHUNK], op=ALU.subtract)
 
         def diff_pool(i):
-            for t0 in range(PACK):
+            for t0 in range(0, PACK, 2):
                 nc.gpsimd.tensor_tensor(
-                    out=z[i][:, t0, :], in0=z[i][:, t0, :], in1=l2s[i][:, t0, :], op=ALU.subtract)
+                    out=z[i][:, t0:t0 + 2, :], in0=z[i][:, t0:t0 + 2, :], in1=l2s[i][:, t0:t0 + 2, :], op=ALU.subtract)
 
         def add_w(i):
+            if i == 1:
+                lo = PE_COLS[1]
+                nc.vector.scalar_tensor_tensor(
+                    out=zflat[1][:, lo:CHUNK], in0=zflat[1][:, lo:CHUNK], scalar=0.5,
+                    in1=w_of[1].rearrange("p t x -> p (t x)")[:, lo:CHUNK], op0=ALU.mult, op1=ALU.add)
+                return
             nc.vector.scalar_tensor_tensor(
                 out=z[i][:], in0=z[i][:], scalar=0.5, in1=w_of[i], op0=ALU.mult, op1=ALU.add)
 
         def tanh(i):
             nc.scalar.activation(out=z[i][:], in_=z[i][:], func=ACT.Tanh)
 
-        z0flat = z[0][:].rearrange("p t x -> p (t x)")
+        zflat = [t[:].rearrange("p t x -> p (t x)") for t in z]
+        PE_COLS = {0: CHUNK, 1: 768}
         with tc.psum_pool(name="zp", bufs=1) as zp:
             zbank = []
             with tc.tile_pool(name="ph1", bufs=2) as ph1:
@@ -114,17 +124,20 @@ def tile_bibayesianconv_kernel(tc, x, weight, epsilon, grad_out, out):
 
                 def logs(i):
                     nc.scalar.activation(out=z[i][:], in_=e_t[i][:], func=ACT.Ln)
-                    l2s[i] = keep.tile([P, PACK, HW], F32, name="l2_%d" % i, tag="l2", bufs=5)
+                    if i in PE_COLS:
+                        l2s[i] = keep.tile([P, PACK, HW], F32, name="l2_%d" % i)
+                    else:
+                        l2s[i] = keep.tile([P, PACK, HW], F32, name="l2_%d" % i, tag="l2", bufs=4)
                     nc.scalar.activation(out=l2s[i][:], in_=e_t[i][:], func=ACT.Ln, scale=-1.0, bias=1.0)
 
-                def pe_z0():
-                    l2flat = l2s[0][:].rearrange("p t x -> p (t x)")
-                    wflat = w_of[0].rearrange("p t x -> p (t x)")
-                    for lo in range(0, CHUNK, NBANK):
-                        hi = min(lo + NBANK, CHUNK)
-                        zb = zp.tile([P, NBANK], F32, name="zb%d" % (lo // NBANK))
-                        zbank.append((zb, lo, hi))
-                        nc.tensor.matmul(out=zb[:, 0:hi - lo], lhsT=halfp[:], rhs=z0flat[:, lo:hi], start=True, stop=False)
+                def pe_z(i):
+                    l2flat = l2s[i][:].rearrange("p t x -> p (t x)")
+                    wflat = w_of[i].rearrange("p t x -> p (t x)")
+                    for lo in range(0, PE_COLS[i], NBANK):
+                        hi = min(lo + NBANK, PE_COLS[i])
+                        zb = zp.tile([P, NBANK], F32, name="zb%d_%d" % (i, lo // NBANK))
+                        zbank.append((i, zb, lo, hi))
+                        nc.tensor.matmul(out=zb[:, 0:hi - lo], lhsT=halfp[:], rhs=zflat[i][:, lo:hi], start=True, stop=False)
                         nc.tensor.matmul(out=zb[:, 0:hi - lo], lhsT=halfn[:], rhs=l2flat[:, lo:hi], start=False, stop=False)
                         nc.tensor.matmul(out=zb[:, 0:hi - lo], lhsT=idb[:], rhs=wflat[:, lo:hi], start=False, stop=True)
 
@@ -141,10 +154,11 @@ def tile_bibayesianconv_kernel(tc, x, weight, epsilon, grad_out, out):
                 load_e(2)
                 load_wh(1)
                 logs(0)
-                pe_z0()
+                pe_z(0)
                 load_e(3)
                 load_w(1)
                 logs(1)
+                pe_z(1)
                 load_e(4)
                 regroup_g(1)
                 quant_g(1)
@@ -179,8 +193,9 @@ def tile_bibayesianconv_kernel(tc, x, weight, epsilon, grad_out, out):
                 regroup_g(5)
                 quant_g(5)
 
-            for zb, lo, hi in zbank:
-                nc.scalar.activation(out=z0flat[:, lo:hi], in_=zb[:, 0:hi - lo], func=ACT.Tanh)
+            for i, zb, lo, hi in zbank:
+                nc.scalar.activation(out=zflat[i][:, lo:hi], in_=zb[:, 0:hi - lo], func=ACT.Tanh)
+            nc.scalar.activation(out=zflat[1][:, PE_COLS[1]:CHUNK], in_=zflat[1][:, PE_COLS[1]:CHUNK], func=ACT.Tanh)
 
         with tc.psum_pool(name="acc", bufs=8) as acc, tc.tile_pool(name="stage", bufs=6) as stg:
             todo = []
@@ -227,7 +242,6 @@ def tile_bibayesianconv_kernel(tc, x, weight, epsilon, grad_out, out):
             diff_pool(5)
             diff_pool(6)
             diff_pool(7)
-            tanh(1)
             tanh(2)
             tanh(3)
             tanh(4)

@@ -68,31 +68,19 @@ def tile_bibayesianconv_kernel(tc, x, weight, epsilon, grad_out, out):
             w_of[2 * m + 1] = t[:, :, HW:2 * HW]
 
         def diff(i):
-            lo = PE_COLS.get(i, 0)
-            nc.vector.tensor_tensor(
-                out=zflat[i][:, lo:CHUNK], in0=zflat[i][:, lo:CHUNK],
-                in1=l2s[i][:].rearrange("p t x -> p (t x)")[:, lo:CHUNK], op=ALU.subtract)
+            nc.vector.tensor_tensor(out=z[i][:], in0=z[i][:], in1=l2s[i][:], op=ALU.subtract)
 
         def diff_pool(i):
-            for t0 in range(0, PACK, 2):
-                nc.gpsimd.tensor_tensor(
-                    out=z[i][:, t0:t0 + 2, :], in0=z[i][:, t0:t0 + 2, :], in1=l2s[i][:, t0:t0 + 2, :], op=ALU.subtract)
+            nc.gpsimd.tensor_tensor(out=z[i][:], in0=z[i][:], in1=l2s[i][:], op=ALU.subtract)
 
         def add_w(i):
-            if i == 1:
-                lo = PE_COLS[1]
-                nc.vector.scalar_tensor_tensor(
-                    out=zflat[1][:, lo:CHUNK], in0=zflat[1][:, lo:CHUNK], scalar=0.5,
-                    in1=w_of[1].rearrange("p t x -> p (t x)")[:, lo:CHUNK], op0=ALU.mult, op1=ALU.add)
-                return
             nc.vector.scalar_tensor_tensor(
                 out=z[i][:], in0=z[i][:], scalar=0.5, in1=w_of[i], op0=ALU.mult, op1=ALU.add)
 
         def tanh(i):
             nc.scalar.activation(out=z[i][:], in_=z[i][:], func=ACT.Tanh)
 
-        zflat = [t[:].rearrange("p t x -> p (t x)") for t in z]
-        PE_COLS = {0: CHUNK, 1: 768}
+        z0flat = z[0][:].rearrange("p t x -> p (t x)")
         with tc.psum_pool(name="zp", bufs=1) as zp:
             zbank = []
             with tc.tile_pool(name="ph1", bufs=2) as ph1:
@@ -124,20 +112,17 @@ def tile_bibayesianconv_kernel(tc, x, weight, epsilon, grad_out, out):
 
                 def logs(i):
                     nc.scalar.activation(out=z[i][:], in_=e_t[i][:], func=ACT.Ln)
-                    if i in PE_COLS:
-                        l2s[i] = keep.tile([P, PACK, HW], F32, name="l2_%d" % i)
-                    else:
-                        l2s[i] = keep.tile([P, PACK, HW], F32, name="l2_%d" % i, tag="l2", bufs=4)
+                    l2s[i] = keep.tile([P, PACK, HW], F32, name="l2_%d" % i, tag="l2", bufs=5)
                     nc.scalar.activation(out=l2s[i][:], in_=e_t[i][:], func=ACT.Ln, scale=-1.0, bias=1.0)
 
-                def pe_z(i):
-                    l2flat = l2s[i][:].rearrange("p t x -> p (t x)")
-                    wflat = w_of[i].rearrange("p t x -> p (t x)")
-                    for lo in range(0, PE_COLS[i], NBANK):
-                        hi = min(lo + NBANK, PE_COLS[i])
-                        zb = zp.tile([P, NBANK], F32, name="zb%d_%d" % (i, lo // NBANK))
-                        zbank.append((i, zb, lo, hi))
-                        nc.tensor.matmul(out=zb[:, 0:hi - lo], lhsT=halfp[:], rhs=zflat[i][:, lo:hi], start=True, stop=False)
+                def pe_z0():
+                    l2flat = l2s[0][:].rearrange("p t x -> p (t x)")
+                    wflat = w_of[0].rearrange("p t x -> p (t x)")
+                    for lo in range(0, CHUNK, NBANK):
+                        hi = min(lo + NBANK, CHUNK)
+                        zb = zp.tile([P, NBANK], F32, name="zb%d" % (lo // NBANK))
+                        zbank.append((zb, lo, hi))
+                        nc.tensor.matmul(out=zb[:, 0:hi - lo], lhsT=halfp[:], rhs=z0flat[:, lo:hi], start=True, stop=False)
                         nc.tensor.matmul(out=zb[:, 0:hi - lo], lhsT=halfn[:], rhs=l2flat[:, lo:hi], start=False, stop=False)
                         nc.tensor.matmul(out=zb[:, 0:hi - lo], lhsT=idb[:], rhs=wflat[:, lo:hi], start=False, stop=True)
 
@@ -154,11 +139,10 @@ def tile_bibayesianconv_kernel(tc, x, weight, epsilon, grad_out, out):
                 load_e(2)
                 load_wh(1)
                 logs(0)
-                pe_z(0)
+                pe_z0()
                 load_e(3)
                 load_w(1)
                 logs(1)
-                pe_z(1)
                 load_e(4)
                 regroup_g(1)
                 quant_g(1)
@@ -193,9 +177,8 @@ def tile_bibayesianconv_kernel(tc, x, weight, epsilon, grad_out, out):
                 regroup_g(5)
                 quant_g(5)
 
-            for i, zb, lo, hi in zbank:
-                nc.scalar.activation(out=zflat[i][:, lo:hi], in_=zb[:, 0:hi - lo], func=ACT.Tanh)
-            nc.scalar.activation(out=zflat[1][:, PE_COLS[1]:CHUNK], in_=zflat[1][:, PE_COLS[1]:CHUNK], func=ACT.Tanh)
+            for zb, lo, hi in zbank:
+                nc.scalar.activation(out=z0flat[:, lo:hi], in_=zb[:, 0:hi - lo], func=ACT.Tanh)
 
         with tc.psum_pool(name="acc", bufs=8) as acc, tc.tile_pool(name="stage", bufs=6) as stg:
             todo = []
@@ -242,6 +225,7 @@ def tile_bibayesianconv_kernel(tc, x, weight, epsilon, grad_out, out):
             diff_pool(5)
             diff_pool(6)
             diff_pool(7)
+            tanh(1)
             tanh(2)
             tanh(3)
             tanh(4)

import concourse.mybir as mybir
from concourse.masks import make_identity

F32 = mybir.dt.float32
BF16 = mybir.dt.bfloat16
U32 = mybir.dt.uint32
U8 = mybir.dt.uint8
E4X4 = mybir.dt.float8_e4m3fn_x4
E5X4 = mybir.dt.float8_e5m2_x4
ACT = mybir.ActivationFunctionType
ALU = mybir.AluOpType
AX = mybir.AxisListType

P = 128
PACK = 4
NF = 512
NC = 512
KK = 9
NB = 2
NPOS = 3072
HC = 64
HW = HC * KK
NCH = NC // HC
GW = 1024
NG = NB * NPOS // GW
NBANK = 512

FLOPS = 2 * NF * NC * NB * NPOS
BYTES = 2 * (NF * NC * KK * 2) + NB * NF * NPOS * 2 + NB * NC * NPOS * 4


def tile_bibayesianconv_kernel(tc, x, weight, epsilon, grad_out, out):
    nc = tc.nc
    w_v = weight.rearrange("(p t) c k l -> p t (c k l)", t=PACK)
    e_v = epsilon.rearrange("s (p t) c k l -> (s p) t (c k l)", t=PACK)
    g_v = grad_out.rearrange("s b (p t) w h -> p (s b) t (w h)", t=PACK)
    o_v = out.rearrange("b (m c) w h -> c b m (w h)", c=P)
    CHUNK = PACK * HW

    with tc.manual_schedule(), tc.tile_pool(name="keep", bufs=1) as keep:
        z = [keep.tile([P, PACK, HW], F32, name="z%d" % i) for i in range(NCH)]
        gq = keep.tile([P, NB * NPOS], U32, name="gq", align_bytes=64)
        gs = keep.tile([P, NB * NPOS], U8, name="gs", align_bytes=64)
        wq = keep.tile([P, NC], U32, name="wq", align_bytes=64)
        ws = keep.tile([P, NC], U8, name="ws", align_bytes=64)
        idf = keep.tile([P, P], F32, name="idf")
        halfp = keep.tile([P, P], F32, name="halfp")
        halfn = keep.tile([P, P], F32, name="halfn")
        idb = keep.tile([P, P], BF16, name="idb")
        w_of = {}
        l2s = {}
        wgrp = {}

        make_identity(nc, idf[:])
        make_identity(nc, idb[:])
        nc.vector.tensor_scalar_mul(out=halfp[:], in0=idf[:], scalar1=0.5)
        nc.vector.tensor_scalar_mul(out=halfn[:], in0=idf[:], scalar1=-0.5)

        def load_wh(i):
            t = keep.tile([P, PACK, HW], BF16, name="wh%d" % i, tag="wh", bufs=2)
            nc.sync.dma_start(out=t[:], in_=w_v[:, :, i * HW:(i + 1) * HW])
            w_of[i] = t[:]

        def load_w(m):
            t = keep.tile([P, PACK, 2 * HW], BF16, name="w%d" % m, tag="w", bufs=2)
            nc.sync.dma_start(out=t[:], in_=w_v[:, :, m * 2 * HW:(m + 1) * 2 * HW])
            w_of[2 * m] = t[:, :, 0:HW]
            w_of[2 * m + 1] = t[:, :, HW:2 * HW]

        def diff(i):
            nc.vector.tensor_tensor(out=z[i][:], in0=z[i][:], in1=l2s[i][:], op=ALU.subtract)

        def diff_pool(i):
            nc.gpsimd.tensor_tensor(out=z[i][:], in0=z[i][:], in1=l2s[i][:], op=ALU.subtract)

        def add_w(i):
            nc.vector.scalar_tensor_tensor(
                out=z[i][:], in0=z[i][:], scalar=0.5, in1=w_of[i], op0=ALU.mult, op1=ALU.add)

        def tanh(i):
            nc.scalar.activation(out=z[i][:], in_=z[i][:], func=ACT.Tanh)

        z0flat = z[0][:].rearrange("p t x -> p (t x)")
        with tc.psum_pool(name="zp", bufs=1) as zp:
            zbank = []
            with tc.tile_pool(name="ph1", bufs=2) as ph1:
                e_t = {}
                graw = {}
                ggrp = {}

                def load_e(i):
                    e_t[i] = ph1.tile([P, PACK, HW], BF16, name="e%d" % i, tag="e", bufs=3)
                    nc.sync.dma_start(out=e_t[i][:], in_=e_v[:, :, i * HW:(i + 1) * HW])

                def load_g(j, lo=0, hi=GW):
                    if lo == 0:
                        graw[j] = ph1.tile([P, PACK, GW], BF16, name="graw%d" % j, tag="graw", bufs=2)
                    b, q = divmod(j, NPOS // GW)
                    nc.sync.dma_start(out=graw[j][:, :, lo:hi], in_=g_v[:, b, :, q * GW + lo:q * GW + hi])

                def regroup_g(j, lo=0, hi=GW):
                    if lo == 0:
                        ggrp[j] = ph1.tile([P, GW, PACK], BF16, name="ggrp%d" % j, tag="ggrp", bufs=2, align_bytes=64)
                    nc.vector.tensor_copy(
                        out=ggrp[j][:, lo:hi, :].rearrange("p (c i) t -> p c t i", i=4),
                        in_=graw[j][:, :, lo:hi].rearrange("p t (c i) -> p c t i", i=4))

                def quant_g(j):
                    nc.vector.quantize_mx(
                        out=gq[:, j * GW:(j + 1) * GW].bitcast(E5X4), scales=gs[:, j * GW:(j + 1) * GW],
                        in_=ggrp[j][:].rearrange("p w t -> p (w t)"))

                def logs(i):
                    nc.scalar.activation(out=z[i][:], in_=e_t[i][:], func=ACT.Ln)
                    l2s[i] = keep.tile([P, PACK, HW], F32, name="l2_%d" % i, tag="l2", bufs=5)
                    nc.scalar.activation(out=l2s[i][:], in_=e_t[i][:], func=ACT.Ln, scale=-1.0, bias=1.0)

                def pe_z0():
                    l2flat = l2s[0][:].rearrange("p t x -> p (t x)")
                    wflat = w_of[0].rearrange("p t x -> p (t x)")
                    for lo in range(0, CHUNK, NBANK):
                        hi = min(lo + NBANK, CHUNK)
                        zb = zp.tile([P, NBANK], F32, name="zb%d" % (lo // NBANK))
                        zbank.append((zb, lo, hi))
                        nc.tensor.matmul(out=zb[:, 0:hi - lo], lhsT=halfp[:], rhs=z0flat[:, lo:hi], start=True, stop=False)
                        nc.tensor.matmul(out=zb[:, 0:hi - lo], lhsT=halfn[:], rhs=l2flat[:, lo:hi], start=False, stop=False)
                        nc.tensor.matmul(out=zb[:, 0:hi - lo], lhsT=idb[:], rhs=wflat[:, lo:hi], start=False, stop=True)

                load_g(0, 0, GW // 2)
                load_e(0)
                load_g(0, GW // 2, GW)
                load_g(1)
                load_e(1)
                load_wh(0)
                regroup_g(0, 0, GW // 2)
                regroup_g(0, GW // 2, GW)
                quant_g(0)
                load_g(2)
                load_e(2)
                load_wh(1)
                logs(0)
                pe_z0()
                load_e(3)
                load_w(1)
                logs(1)
                load_e(4)
                regroup_g(1)
                quant_g(1)
                load_g(3)
                logs(2)
                load_e(5)
                load_w(2)
                logs(3)
                load_e(6)
                regroup_g(2)
                load_g(4)
                logs(4)
                load_e(7)
                diff(1)
                quant_g(2)
                add_w(1)
                diff(2)
                add_w(2)
                regroup_g(3)
                load_g(5)
                diff(3)
                quant_g(3)
                add_w(3)
                load_w(3)
                logs(5)
                logs(6)
                logs(7)
                regroup_g(4)
                diff(4)
                quant_g(4)
                add_w(4)
                regroup_g(5)
                quant_g(5)

            for zb, lo, hi in zbank:
                nc.scalar.activation(out=z0flat[:, lo:hi], in_=zb[:, 0:hi - lo], func=ACT.Tanh)

        with tc.psum_pool(name="acc", bufs=8) as acc, tc.tile_pool(name="stage", bufs=6) as stg:
            todo = []
            state = {}

            def sum9(i):
                m, h = divmod(i, 2)
                if h == 0:
                    wgrp[m] = keep.tile([P, P, PACK], BF16, name="wgrp%d" % m, tag="wgrp", bufs=2, align_bytes=64)
                with nc.allow_low_precision(reason="the float32 sum of 9 is rounded once to bfloat16 on the way out"):
                    nc.vector.tensor_reduce(
                        out=wgrp[m][:, h * HC:(h + 1) * HC, :].rearrange("p c t -> p t c"),
                        in_=z[i][:].rearrange("p t (c k) -> p t c k", k=KK), axis=AX.X, op=ALU.add)

            def quant_w(m):
                cols = slice(m * P, (m + 1) * P)
                nc.vector.quantize_mx(
                    out=wq[:, cols].bitcast(E4X4), scales=ws[:, cols],
                    in_=wgrp[m][:].rearrange("p c t -> p (c t)"))
                for n in range(NB * NPOS // NBANK):
                    todo.append((m, n))

            def drain(engines):
                for r in range(len(engines)):
                    m, n = todo.pop(0)
                    cols = slice(m * P, (m + 1) * P)
                    if n % 2 == 0:
                        state["st"] = stg.tile([P, 2 * NBANK], F32, name="st", tag="st")
                    st = state["st"]
                    ps = acc.tile([P, NBANK], F32, name="ps", tag="ps")
                    nc.tensor.matmul_mx(
                        out=ps[:], lhsT=wq[:, cols].bitcast(E4X4), lhsT_scale=ws[:, cols],
                        rhs=gq[:, n * NBANK:(n + 1) * NBANK].bitcast(E5X4), rhs_scale=gs[:, n * NBANK:(n + 1) * NBANK],
                        start=True, stop=True)
                    half = st[:, (n % 2) * NBANK:(n % 2 + 1) * NBANK]
                    if engines[r] == "v":
                        nc.vector.tensor_copy(out=half, in_=ps[:])
                    else:
                        nc.scalar.copy(out=half, in_=ps[:])
                    if n % 2 == 1:
                        b, q = divmod(n // 2, NPOS // (2 * NBANK))
                        nc.sync.dma_start(out=o_v[:, b, m, q * 2 * NBANK:(q + 1) * 2 * NBANK], in_=st[:])

            diff_pool(5)
            diff_pool(6)
            diff_pool(7)
            tanh(1)
            tanh(2)
            tanh(3)
            tanh(4)
            sum9(0)
            sum9(1)
            quant_w(0)
            add_w(5)
            drain("s" * 12)
            sum9(2)
            sum9(3)
            quant_w(1)
            add_w(6)
            drain("ss")
            tanh(5)
            sum9(4)
            drain("svsvv")
            sum9(5)
            quant_w(2)
            drain("sss")
            tanh(6)
            drain("v")
            add_w(7)
            drain("s" * 5)
            tanh(7)
            drain("vv")
            sum9(6)
            drain("s" * 6)
            sum9(7)
            quant_w(3)
            drain("sv" * 6)
